import numpy as np
import ml_dtypes


def mxq(x, axis, fmt="e4m3"):
    dtype, down = {"e4m3": (ml_dtypes.float8_e4m3fn, 7), "e5m2": (ml_dtypes.float8_e5m2, 14)}[fmt]
    v = np.moveaxis(np.asarray(x, np.float32).astype(ml_dtypes.bfloat16).astype(np.float64), axis, -1)
    blocks = v.reshape(v.shape[:-1] + (-1, 32))
    amax = np.abs(blocks).max(-1, keepdims=True)
    byte = np.maximum(np.where(amax > 0, np.frexp(amax)[1] - 1 + 127, 0) - down, 1)
    scale = np.exp2(byte - 127.0)
    codes = (blocks / scale).astype(np.float32).astype(dtype).astype(np.float64)
    return np.moveaxis((codes * scale).reshape(v.shape), -1, axis)


WIDE = False


def mx_kscale(k):
    if not WIDE:
        return np.ones(k)
    levels = np.array([10, -10, 5, -5, 0])
    a = np.random.permutation(np.resize(levels, k // 512 * 4)).reshape(k // 512, 4)
    idx = np.arange(k)
    return np.exp2(a[idx // 512, idx % 128 // 32])


BF16 = ml_dtypes.bfloat16


def bf(x):
    return np.asarray(x, np.float32).astype(BF16)


def f64(x):
    return np.asarray(x).astype(np.float64)


NO, CENTERS, C, VD, H, W = 4, 2048, 256, 512, 16, 24
HW = H * W
KEY_SCALE = 2.0
VAL_SCALE = 2.0


def setup_inputs():
    s = mx_kscale(CENTERS)
    shift = np.log2(s) * np.log(2.0)
    m_in = np.random.standard_normal((NO, CENTERS, C)) * KEY_SCALE
    m_out = np.random.standard_normal((NO, CENTERS, VD)) * VAL_SCALE
    q_in = np.random.standard_normal((NO, C, H, W))
    p_m_in = np.random.standard_normal((NO, CENTERS, C)) * KEY_SCALE
    p_q_in = np.random.standard_normal((NO, C, H, W))
    q_in[:, 0] = np.sqrt(C)
    p_q_in[:, 0] = np.sqrt(C)
    m_in[:, :, 0] = m_in[:, :, 0] / np.sqrt(C) + shift[None, :]
    p_m_in[:, :, 0] = p_m_in[:, :, 0] / np.sqrt(C) + shift[None, :]
    m_out = m_out / s[None, :, None] * s.mean()
    return {"m_in": bf(m_in), "m_out": bf(m_out), "q_in": bf(q_in), "p_m_in": bf(p_m_in), "p_q_in": bf(p_q_in)}


def reference(m_in, m_out, q_in, p_m_in, p_q_in):
    s = f64(m_in) @ f64(q_in).reshape(NO, C, HW) / np.sqrt(C)
    e = np.exp(s - s.max(1, keepdims=True))
    s_p = f64(p_m_in) @ f64(p_q_in).reshape(NO, C, HW) / np.sqrt(C)
    e_p = np.exp(s_p - s_p.max(1, keepdims=True))
    vq = mxq(f64(m_out), 1, "e4m3").transpose(0, 2, 1)
    mem = ((vq @ mxq(e, 1, "e4m3")) / e.sum(1, keepdims=True)).reshape(NO, VD, H, W)
    mem_p = ((vq @ mxq(e_p, 1, "e4m3")) / e_p.sum(1, keepdims=True)).reshape(NO, VD, H, W)
    return mem + mem_p

@@ -1,0 +1,336 @@
+from contextlib import ExitStack
+
+import concourse.bass as bass
+import concourse.mybir as mybir
+import concourse.tile as tile
+from concourse.masks import make_identity
+
+F32 = mybir.dt.float32
+BF16 = mybir.dt.bfloat16
+U32 = mybir.dt.uint32
+U8 = mybir.dt.uint8
+FP8X4 = mybir.dt.float8_e4m3fn_x4
+ALU = mybir.AluOpType
+ACT = mybir.ActivationFunctionType
+AX = mybir.AxisListType
+
+P = 128
+NO, CENTERS, C, VD, HW = 4, 2048, 256, 512, 384
+G = CENTERS // 512
+XT = HW // P
+U = NO * 2 * XT
+FLOPS = 2 * NO * 2 * CENTERS * C * HW + 2 * NO * 2 * VD * CENTERS * HW
+
+
+def tile_memory_pa_kernel(tc, m_in, m_out, q_in, p_m_in, p_q_in, out):
+    nc = tc.nc
+    keys = [m_in, p_m_in]
+    queries = [q_in, p_q_in]
+    with ExitStack() as ctx:
+        const = ctx.enter_context(tc.tile_pool(name="const", bufs=1))
+        xin = ctx.enter_context(tc.tile_pool(name="xin", bufs=3))
+        tpool = ctx.enter_context(tc.tile_pool(name="tpool", bufs=2))
+        rpool = ctx.enter_context(tc.tile_pool(name="rpool", bufs=2))
+        vgp = ctx.enter_context(tc.tile_pool(name="vgp", bufs=2))
+        vwp = ctx.enter_context(tc.tile_pool(name="vwp", bufs=2))
+        scp = ctx.enter_context(tc.tile_pool(name="scp", bufs=3))
+        ep = ctx.enter_context(tc.tile_pool(name="ep", bufs=3))
+        egp = ctx.enter_context(tc.tile_pool(name="egp", bufs=2))
+        ewp = ctx.enter_context(tc.tile_pool(name="ewp", bufs=3))
+        small = ctx.enter_context(tc.tile_pool(name="small", bufs=8))
+        t1p = ctx.enter_context(tc.tile_pool(name="t1p", bufs=5))
+        t2p = ctx.enter_context(tc.tile_pool(name="t2p", bufs=2))
+        osp = ctx.enter_context(tc.tile_pool(name="osp", bufs=2))
+        ps_s = ctx.enter_context(tc.psum_pool(name="ps_s", bufs=3))
+        ps_e = ctx.enter_context(tc.psum_pool(name="ps_e", bufs=2))
+        ps_a = ctx.enter_context(tc.psum_pool(name="ps_a", bufs=1))
+        ps_t = ctx.enter_context(tc.psum_pool(name="ps_t", bufs=2))
+        ctx.enter_context(tc.manual_schedule())
+
+        ident_f = const.tile([P, P], F32, name="ident_f")
+        make_identity(nc, ident_f[:])
+        ident_b = const.tile([P, P], BF16, name="ident_b")
+        make_identity(nc, ident_b[:])
+        warm = const.tile([P, 8], F32, name="warm")
+        nc.vector.memset(warm[:], 0.0)
+        nc.scalar.activation(out=warm[:], in_=warm[:], func=ACT.Exp)
+
+        st = {}
+
+        def load_q(nb):
+            n, b = divmod(nb, 2)
+            q = const.tile([P, 2, HW], BF16, name="q%d" % nb)
+            nc.sync.dma_start(out=q[:], in_=queries[b][n].rearrange("(w e) h v -> w e (h v)", e=2))
+            st["q", nb] = q
+
+        def load_x(nb):
+            n, b = divmod(nb, 2)
+            x = xin.tile([P, G * 1024], BF16, name="x", tag="x")
+            nc.sync.dma_start(
+                out=x[:].rearrange("j (g k) -> j g k", g=G),
+                in_=keys[b][n].rearrange("(g j r) c -> j g (r c)", g=G, r=4),
+            )
+            st["x", nb] = x
+
+        def load_r(n):
+            r = rpool.tile([P, G * 2048], BF16, name="r", tag="r")
+            nc.sync.dma_start(
+                out=r[:].rearrange("p (g k) -> p g k", g=G),
+                in_=m_out[n].rearrange("(g p t) w -> p g (t w)", g=G, t=4),
+            )
+            st["r", n] = r
+
+        def tm_steps(nb, g):
+            steps = []
+
+            def one(r):
+                def go():
+                    if r == 0:
+                        if g == 0:
+                            st["T", nb] = tpool.tile([P, CENTERS], F32, name="T", tag="T")
+                        st["tmb", nb] = ps_t.tile([P, 512], F32, name="tb", tag="tb")
+                    xw = st["x", nb][:].bitcast(F32)
+                    nc.tensor.transpose(
+                        st["tmb", nb][:, r * P : (r + 1) * P],
+                        xw[:, (g * 4 + r) * P : (g * 4 + r + 1) * P],
+                        ident_f[:],
+                    )
+                    if r == 3:
+                        nc.vector.tensor_copy(
+                            out=st["T", nb][:, g * 512 : (g + 1) * 512], in_=st["tmb", nb][:]
+                        )
+                return go
+
+            for r in range(4):
+                steps.append(one(r))
+            return steps
+
+        def te_steps(u):
+            steps = []
+
+            def one(i):
+                def go():
+                    h, k = divmod(i, 8)
+                    if i == 0:
+                        st["eg", u] = egp.tile([P, 2048], BF16, name="eg", tag="eg", align_bytes=64)
+                    if k == 0:
+                        st["eT", u] = ps_e.tile([P, 1024], BF16, name="eT", tag="eT")
+                    nc.tensor.transpose(
+                        st["eT", u][:, k * P : (k + 1) * P],
+                        st["e", u][:, i * P : (i + 1) * P],
+                        ident_b[:],
+                    )
+                    if k == 7:
+                        nc.scalar.copy(
+                            out=st["eg", u][:, h * 1024 : (h + 1) * 1024].rearrange(
+                                "p (g x t) -> p g x t", g=2, t=4
+                            ),
+                            in_=st["eT", u][:].rearrange("p (g t x) -> p g x t", g=2, t=4),
+                        )
+                return go
+
+            for i in range(16):
+                steps.append(one(i))
+            return steps
+
+        def to_steps(u):
+            n, rest = divmod(u, 6)
+            t = rest - 3
+            steps = []
+
+            def one(v):
+                def go():
+                    if v == 0:
+                        st["ob", u] = ps_t.tile([P, 512], F32, name="tb", tag="tb")
+                        if t == 0:
+                            st["os", n] = osp.tile([P, 4, HW], F32, name="os", tag="os")
+                    nc.tensor.transpose(
+                        st["ob", u][:, v * P : (v + 1) * P],
+                        st["t2", u][:, v * P : (v + 1) * P],
+                        ident_f[:],
+                    )
+                    if v == 3:
+                        nc.scalar.copy(
+                            out=st["os", n][:, :, t * P : (t + 1) * P],
+                            in_=st["ob", u][:].rearrange("p (v x) -> p v x", v=4),
+                        )
+                        if t == XT - 1:
+                            nc.sync.dma_start(
+                                out=out[n].rearrange("(v p) h w -> p v (h w)", v=4),
+                                in_=st["os", n][:],
+                            )
+                return go
+
+            for v in range(4):
+                steps.append(one(v))
+            return steps
+
+        def merge(a, b):
+            res = []
+            na, nb_ = len(a), len(b)
+            ia = ib = 0
+            while ia < na or ib < nb_:
+                if ib >= nb_ or (ia < na and ia * nb_ <= ib * na):
+                    res.append(a[ia])
+                    ia += 1
+                else:
+                    res.append(b[ib])
+                    ib += 1
+            return res
+
+        def scores(u, fill):
+            nb, t = divmod(u, XT)
+            sc = scp.tile([P, CENTERS], F32, name="sc", tag="sc")
+            mx4 = small.tile([P, G], F32, name="mx4", tag="mx4")
+            t2v = st["T", nb][:].bitcast(BF16).rearrange("w (k e) -> w k e", e=2)
+            q = st["q", nb]
+            per = -(-len(fill) // 7)
+            pos = 0
+            for g in range(G):
+                bank = ps_s.tile([P, 512], F32, name="sb", tag="sb")
+                for e in range(2):
+                    nc.tensor.matmul(
+                        out=bank[:],
+                        lhsT=q[:, e, t * P : (t + 1) * P],
+                        rhs=t2v[:, g * 512 : (g + 1) * 512, e],
+                        start=(e == 0),
+                        stop=(e == 1),
+                    )
+                    if e == 1:
+                        nc.vector.tensor_scalar(
+                            out=sc[:, g * 512 : (g + 1) * 512],
+                            in0=bank[:],
+                            scalar1=1.0 / 16.0,
+                            scalar2=None,
+                            op0=ALU.mult,
+                            op1=ALU.max,
+                            accum_out=mx4[:, g : g + 1],
+                        )
+                    if not (g == G - 1 and e == 1):
+                        for f in fill[pos : pos + per]:
+                            f()
+                        pos += per
+            nmx = small.tile([P, 1], F32, name="nmx", tag="nmx")
+            nc.vector.tensor_reduce(out=nmx[:], in_=mx4[:], axis=AX.X, op=ALU.max, negate=True)
+            e_t = ep.tile([P, CENTERS], BF16, name="e", tag="e")
+            cs = small.tile([P, 1], F32, name="cs", tag="cs")
+            nc.scalar.activation(
+                out=e_t[:], in_=sc[:], func=ACT.Exp, bias=nmx[:], scale=1.0, accum_out=cs[:]
+            )
+            st["e", u] = e_t
+            st["cs", u] = cs
+
+        def recip(u):
+            rc = small.tile([P, 1], F32, name="rc", tag="rc")
+            nc.vector.reciprocal(out=rc[:], in_=st["cs", u][:])
+            st["rc", u] = rc
+
+        def quant_e(u):
+            ew = ewp.tile([P, 512], U32, name="ew", tag="ew", align_bytes=64)
+            es = ewp.tile([P, 512], U8, name="es", tag="es", align_bytes=64)
+            nc.vector.quantize_mx(out=ew[:].bitcast(FP8X4), scales=es[:], in_=st["eg", u][:])
+            st["ew", u] = ew
+            st["es", u] = es
+
+        def readout(u):
+            n, rest = divmod(u, 6)
+            b, t = divmod(rest, XT)
+            acc = ps_a.tile([P, VD], F32, name="acc", tag="acc")
+            ew, es = st["ew", u], st["es", u]
+            vw, vs = st["vw", n], st["vs", n]
+            for g in range(G):
+                nc.tensor.matmul_mx(
+                    out=acc[:],
+                    lhsT=ew[:, g * P : (g + 1) * P].bitcast(FP8X4),
+                    lhsT_scale=es[:, g * P : (g + 1) * P],
+                    rhs=vw[:, g * 512 : (g + 1) * 512].bitcast(FP8X4),
+                    rhs_scale=vs[:, g * 512 : (g + 1) * 512],
+                    start=(g == 0),
+                    stop=(g == G - 1),
+                )
+            if b == 0:
+                t1 = t1p.tile([P, VD], F32, name="t1", tag="t1")
+                nc.scalar.activation(out=t1[:], in_=acc[:], func=ACT.Copy, scale=st["rc", u][:])
+                st["t1", u] = t1
+            else:
+                t2 = t2p.tile([P, VD], F32, name="t2", tag="t2")
+                nc.vector.scalar_tensor_tensor(
+                    out=t2[:],
+                    in0=acc[:],
+                    scalar=st["rc", u][:],
+                    in1=st["t1", u - XT][:],
+                    op0=ALU.mult,
+                    op1=ALU.add,
+                )
+                st["t2", u] = t2
+
+        def values_regroup(n, g):
+            if g == 0:
+                st["vw", n] = vwp.tile([P, G * 512], U32, name="vw", tag="vw", align_bytes=64)
+                st["vs", n] = vwp.tile([P, G * 512], U8, name="vs", tag="vs", align_bytes=64)
+            vg = vgp.tile([P, 2048], BF16, name="vg", tag="vg", align_bytes=64)
+            nc.vector.tensor_copy(
+                out=vg[:].rearrange("p (c i t) -> p c t i", i=4, t=4),
+                in_=st["r", n][:, g * 2048 : (g + 1) * 2048].rearrange(
+                    "p (t c i) -> p c t i", t=4, i=4
+                ),
+            )
+            st["vg", n, g] = vg
+
+        def values_quant(n, g):
+            nc.vector.quantize_mx(
+                out=st["vw", n][:, g * 512 : (g + 1) * 512].bitcast(FP8X4),
+                scales=st["vs", n][:, g * 512 : (g + 1) * 512],
+                in_=st["vg", n, g][:],
+            )
+
+        vslot = {}
+        for n in range(NO):
+            for g in range(G):
+                s = 6 * n - 3 + g if n > 0 else [0, 0, 1, 2][g]
+                vslot[s] = vslot.get(s, []) + [(n, g)]
+
+        load_q(0)
+        load_x(0)
+        load_q(1)
+        load_x(1)
+        load_r(0)
+        load_x(2)
+        load_q(2)
+        for g in range(G):
+            for f in tm_steps(0, g):
+                f()
+
+        for s in range(U + 6):
+            if s % 3 == 0 and s // 3 + 3 < 2 * NO:
+                load_q(s // 3 + 3)
+                load_x(s // 3 + 3)
+            if s % 6 == 0 and s // 6 + 1 < NO:
+                load_r(s // 6 + 1)
+            fa = te_steps(s - 2) if 0 <= s - 2 < U else []
+            fb = []
+            nbn = s // 3 + 1
+            if nbn < 2 * NO:
+                if s % 3 == 0:
+                    fb += tm_steps(nbn, 0) + tm_steps(nbn, 1)
+                else:
+                    fb += tm_steps(nbn, s % 3 + 1)
+            if 0 <= s - 4 < U and (s - 4) % 6 >= 3:
+                fb += to_steps(s - 4)
+            fill = merge(fa, fb)
+            if s < U:
+                scores(s, fill)
+            else:
+                for f in fill:
+                    f()
+            if 0 <= s - 1 < U:
+                recip(s - 1)
+            vch = vslot.get(s, [])
+            for (n, g) in vch:
+                values_regroup(n, g)
+            if 0 <= s - 2 < U:
+                quant_e(s - 2)
+            for (n, g) in vch:
+                values_quant(n, g)
+            if 0 <= s - 3 < U:
+                readout(s - 3)

@@ -1,8 +1,6 @@
 from contextlib import ExitStack
 
-import concourse.bass as bass
 import concourse.mybir as mybir
-import concourse.tile as tile
 from concourse.masks import make_identity
 
 F32 = mybir.dt.float32
@@ -20,6 +18,8 @@ G = CENTERS // 512
 XT = HW // P
 U = NO * 2 * XT
 FLOPS = 2 * NO * 2 * CENTERS * C * HW + 2 * NO * 2 * VD * CENTERS * HW
+VALUES_ON_GPSIMD = True
+N1_ON_VECTOR = True
 
 
 def tile_memory_pa_kernel(tc, m_in, m_out, q_in, p_m_in, p_q_in, out):
@@ -31,7 +31,7 @@ def tile_memory_pa_kernel(tc, m_in, m_out, q_in, p_m_in, p_q_in, out):
         xin = ctx.enter_context(tc.tile_pool(name="xin", bufs=3))
         tpool = ctx.enter_context(tc.tile_pool(name="tpool", bufs=2))
         rpool = ctx.enter_context(tc.tile_pool(name="rpool", bufs=2))
-        vgp = ctx.enter_context(tc.tile_pool(name="vgp", bufs=2))
+        vgp = ctx.enter_context(tc.tile_pool(name="vgp", bufs=1))
         vwp = ctx.enter_context(tc.tile_pool(name="vwp", bufs=2))
         scp = ctx.enter_context(tc.tile_pool(name="scp", bufs=3))
         ep = ctx.enter_context(tc.tile_pool(name="ep", bufs=3))
@@ -47,14 +47,6 @@ def tile_memory_pa_kernel(tc, m_in, m_out, q_in, p_m_in, p_q_in, out):
         ps_t = ctx.enter_context(tc.psum_pool(name="ps_t", bufs=2))
         ctx.enter_context(tc.manual_schedule())
 
-        ident_f = const.tile([P, P], F32, name="ident_f")
-        make_identity(nc, ident_f[:])
-        ident_b = const.tile([P, P], BF16, name="ident_b")
-        make_identity(nc, ident_b[:])
-        warm = const.tile([P, 8], F32, name="warm")
-        nc.vector.memset(warm[:], 0.0)
-        nc.scalar.activation(out=warm[:], in_=warm[:], func=ACT.Exp)
-
         st = {}
 
         def load_q(nb):
@@ -63,26 +55,28 @@ def tile_memory_pa_kernel(tc, m_in, m_out, q_in, p_m_in, p_q_in, out):
             nc.sync.dma_start(out=q[:], in_=queries[b][n].rearrange("(w e) h v -> w e (h v)", e=2))
             st["q", nb] = q
 
-        def load_x(nb):
+        def load_x(nb, pieces):
             n, b = divmod(nb, 2)
             x = xin.tile([P, G * 1024], BF16, name="x", tag="x")
-            nc.sync.dma_start(
-                out=x[:].rearrange("j (g k) -> j g k", g=G),
-                in_=keys[b][n].rearrange("(g j r) c -> j g (r c)", g=G, r=4),
-            )
+            src = keys[b][n].rearrange("(g j r) c -> j g (r c)", g=G, r=4)
+            dst = x[:].rearrange("j (g k) -> j g k", g=G)
+            step = G // pieces
+            for i in range(pieces):
+                nc.sync.dma_start(
+                    out=dst[:, i * step : (i + 1) * step, :], in_=src[:, i * step : (i + 1) * step, :]
+                )
             st["x", nb] = x
 
-        def load_r(n):
-            r = rpool.tile([P, G * 2048], BF16, name="r", tag="r")
+        def alloc_r(n):
+            st["r", n] = rpool.tile([P, G * 2048], BF16, name="r", tag="r")
+
+        def load_r(n, g0, g1):
             nc.sync.dma_start(
-                out=r[:].rearrange("p (g k) -> p g k", g=G),
-                in_=m_out[n].rearrange("(g p t) w -> p g (t w)", g=G, t=4),
+                out=st["r", n][:].rearrange("p (g k) -> p g k", g=G)[:, g0:g1, :],
+                in_=m_out[n].rearrange("(g p t) w -> p g (t w)", g=G, t=4)[:, g0:g1, :],
             )
-            st["r", n] = r
 
-        def tm_steps(nb, g):
-            steps = []
-
+        def tm_steps(nb, g, on_vector):
             def one(r):
                 def go():
                     if r == 0:
@@ -96,47 +90,45 @@ def tile_memory_pa_kernel(tc, m_in, m_out, q_in, p_m_in, p_q_in, out):
                         ident_f[:],
                     )
                     if r == 3:
-                        nc.vector.tensor_copy(
-                            out=st["T", nb][:, g * 512 : (g + 1) * 512], in_=st["tmb", nb][:]
+                        dst = st["T", nb][:, g * 512 : (g + 1) * 512].rearrange(
+                            "w (u j e) -> w u j e", u=2, e=2
                         )
+                        src = st["tmb", nb][:].rearrange("w (u e j) -> w u j e", u=2, e=2)
+                        if on_vector:
+                            nc.vector.tensor_copy(out=dst, in_=src)
+                        else:
+                            nc.scalar.copy(out=dst, in_=src)
                 return go
 
-            for r in range(4):
-                steps.append(one(r))
-            return steps
+            return [one(r) for r in range(4)]
 
         def te_steps(u):
-            steps = []
-
             def one(i):
                 def go():
-                    h, k = divmod(i, 8)
+                    h, k = divmod(i, 4)
                     if i == 0:
                         st["eg", u] = egp.tile([P, 2048], BF16, name="eg", tag="eg", align_bytes=64)
                     if k == 0:
-                        st["eT", u] = ps_e.tile([P, 1024], BF16, name="eT", tag="eT")
+                        st["eT", u] = ps_e.tile([P, 512], F32, name="eT", tag="eT")
                     nc.tensor.transpose(
                         st["eT", u][:, k * P : (k + 1) * P],
-                        st["e", u][:, i * P : (i + 1) * P],
-                        ident_b[:],
+                        st["e", u][:].bitcast(F32)[:, i * P : (i + 1) * P],
+                        ident_f[:],
                     )
-                    if k == 7:
+                    if k == 3:
                         nc.scalar.copy(
-                            out=st["eg", u][:, h * 1024 : (h + 1) * 1024].rearrange(
-                                "p (g x t) -> p g x t", g=2, t=4
+                            out=st["eg", u][:].bitcast(F32)[:, h * 512 : (h + 1) * 512].rearrange(
+                                "p (g x u) -> p g x u", g=2, u=2
                             ),
-                            in_=st["eT", u][:].rearrange("p (g t x) -> p g x t", g=2, t=4),
+                            in_=st["eT", u][:].rearrange("p (g u x) -> p g x u", g=2, u=2),
                         )
                 return go
 
-            for i in range(16):
-                steps.append(one(i))
-            return steps
+            return [one(i) for i in range(8)]
 
         def to_steps(u):
             n, rest = divmod(u, 6)
             t = rest - 3
-            steps = []
 
             def one(v):
                 def go():
@@ -161,9 +153,7 @@ def tile_memory_pa_kernel(tc, m_in, m_out, q_in, p_m_in, p_q_in, out):
                             )
                 return go
 
-            for v in range(4):
-                steps.append(one(v))
-            return steps
+            return [one(v) for v in range(4)]
 
         def merge(a, b):
             res = []
@@ -184,8 +174,7 @@ def tile_memory_pa_kernel(tc, m_in, m_out, q_in, p_m_in, p_q_in, out):
             mx4 = small.tile([P, G], F32, name="mx4", tag="mx4")
             t2v = st["T", nb][:].bitcast(BF16).rearrange("w (k e) -> w k e", e=2)
             q = st["q", nb]
-            per = -(-len(fill) // 7)
-            pos = 0
+            gaps = 2 * G - 1
             for g in range(G):
                 bank = ps_s.tile([P, 512], F32, name="sb", tag="sb")
                 for e in range(2):
@@ -206,10 +195,10 @@ def tile_memory_pa_kernel(tc, m_in, m_out, q_in, p_m_in, p_q_in, out):
                             op1=ALU.max,
                             accum_out=mx4[:, g : g + 1],
                         )
-                    if not (g == G - 1 and e == 1):
-                        for f in fill[pos : pos + per]:
+                    i = 2 * g + e
+                    if i < gaps:
+                        for f in fill[i * len(fill) // gaps : (i + 1) * len(fill) // gaps]:
                             f()
-                        pos += per
             nmx = small.tile([P, 1], F32, name="nmx", tag="nmx")
             nc.vector.tensor_reduce(out=nmx[:], in_=mx4[:], axis=AX.X, op=ALU.max, negate=True)
             e_t = ep.tile([P, CENTERS], BF16, name="e", tag="e")
@@ -250,7 +239,12 @@ def tile_memory_pa_kernel(tc, m_in, m_out, q_in, p_m_in, p_q_in, out):
                 )
             if b == 0:
                 t1 = t1p.tile([P, VD], F32, name="t1", tag="t1")
-                nc.scalar.activation(out=t1[:], in_=acc[:], func=ACT.Copy, scale=st["rc", u][:])
+                if N1_ON_VECTOR:
+                    nc.vector.tensor_scalar(
+                        out=t1[:], in0=acc[:], scalar1=st["rc", u][:], scalar2=None, op0=ALU.mult
+                    )
+                else:
+                    nc.scalar.activation(out=t1[:], in_=acc[:], func=ACT.Copy, scale=st["rc", u][:])
                 st["t1", u] = t1
             else:
                 t2 = t2p.tile([P, VD], F32, name="t2", tag="t2")
@@ -265,19 +259,29 @@ def tile_memory_pa_kernel(tc, m_in, m_out, q_in, p_m_in, p_q_in, out):
                 st["t2", u] = t2
 
         def values_regroup(n, g):
-            if g == 0:
-                st["vw", n] = vwp.tile([P, G * 512], U32, name="vw", tag="vw", align_bytes=64)
-                st["vs", n] = vwp.tile([P, G * 512], U8, name="vs", tag="vs", align_bytes=64)
             vg = vgp.tile([P, 2048], BF16, name="vg", tag="vg", align_bytes=64)
-            nc.vector.tensor_copy(
-                out=vg[:].rearrange("p (c i t) -> p c t i", i=4, t=4),
-                in_=st["r", n][:, g * 2048 : (g + 1) * 2048].rearrange(
-                    "p (t c i) -> p c t i", t=4, i=4
-                ),
-            )
+            if VALUES_ON_GPSIMD:
+                nc.gpsimd.tensor_scalar(
+                    out=vg[:].rearrange("p (w t) -> p w t", t=4),
+                    in0=st["r", n][:, g * 2048 : (g + 1) * 2048].rearrange("p (t w) -> p w t", t=4),
+                    scalar1=1.0,
+                    scalar2=0.0,
+                    op0=ALU.mult,
+                    op1=ALU.add,
+                )
+            else:
+                nc.vector.tensor_copy(
+                    out=vg[:].rearrange("p (c i t) -> p c t i", i=4, t=4),
+                    in_=st["r", n][:, g * 2048 : (g + 1) * 2048].rearrange(
+                        "p (t c i) -> p c t i", t=4, i=4
+                    ),
+                )
             st["vg", n, g] = vg
 
         def values_quant(n, g):
+            if g == 0:
+                st["vw", n] = vwp.tile([P, G * 512], U32, name="vw", tag="vw", align_bytes=64)
+                st["vs", n] = vwp.tile([P, G * 512], U8, name="vs", tag="vs", align_bytes=64)
             nc.vector.quantize_mx(
                 out=st["vw", n][:, g * 512 : (g + 1) * 512].bitcast(FP8X4),
                 scales=st["vs", n][:, g * 512 : (g + 1) * 512],
@@ -285,38 +289,50 @@ def tile_memory_pa_kernel(tc, m_in, m_out, q_in, p_m_in, p_q_in, out):
             )
 
         vslot = {}
-        for n in range(NO):
-            for g in range(G):
-                s = 6 * n - 3 + g if n > 0 else [0, 0, 1, 2][g]
-                vslot[s] = vslot.get(s, []) + [(n, g)]
+        chunks = [(n, g) for n in range(NO) for g in range(G)]
+        for (n, g) in chunks:
+            vslot[6 * n - 2 + g if n > 0 else g] = (n, g)
 
         load_q(0)
-        load_x(0)
+        load_x(0, 4)
+        alloc_r(0)
+        load_r(0, 0, 1)
         load_q(1)
-        load_x(1)
-        load_r(0)
-        load_x(2)
+        load_x(1, 2)
+        load_r(0, 1, 4)
         load_q(2)
+        load_x(2, 1)
+        ident_f = const.tile([P, P], F32, name="ident_f")
+        make_identity(nc, ident_f[:])
+        warm = const.tile([P, 8], F32, name="warm")
+        nc.vector.memset(warm[:], 0.0)
+        nc.scalar.activation(out=warm[:], in_=warm[:], func=ACT.Exp)
         for g in range(G):
-            for f in tm_steps(0, g):
+            for f in tm_steps(0, g, g % 2 == 0):
                 f()
+        values_regroup(0, 0)
+
+        tm_queue = []
+        for nb in range(1, 2 * NO):
+            for g in range(G):
+                tm_queue += tm_steps(nb, g, False)
+        tm_count = [8, 4, 4, 4, 6, 6]
+        tm_pos = 0
 
         for s in range(U + 6):
             if s % 3 == 0 and s // 3 + 3 < 2 * NO:
                 load_q(s // 3 + 3)
-                load_x(s // 3 + 3)
+                load_x(s // 3 + 3, 1)
             if s % 6 == 0 and s // 6 + 1 < NO:
-                load_r(s // 6 + 1)
+                alloc_r(s // 6 + 1)
+                load_r(s // 6 + 1, 0, 4)
             fa = te_steps(s - 2) if 0 <= s - 2 < U else []
             fb = []
-            nbn = s // 3 + 1
-            if nbn < 2 * NO:
-                if s % 3 == 0:
-                    fb += tm_steps(nbn, 0) + tm_steps(nbn, 1)
-                else:
-                    fb += tm_steps(nbn, s % 3 + 1)
             if 0 <= s - 4 < U and (s - 4) % 6 >= 3:
                 fb += to_steps(s - 4)
+            k = [0, 8, 8][s] if s < 3 else tm_count[s % 6]
+            fb += tm_queue[tm_pos : tm_pos + k]
+            tm_pos += k
             fill = merge(fa, fb)
             if s < U:
                 scores(s, fill)
@@ -325,12 +341,13 @@ def tile_memory_pa_kernel(tc, m_in, m_out, q_in, p_m_in, p_q_in, out):
                     f()
             if 0 <= s - 1 < U:
                 recip(s - 1)
-            vch = vslot.get(s, [])
-            for (n, g) in vch:
-                values_regroup(n, g)
             if 0 <= s - 2 < U:
                 quant_e(s - 2)
-            for (n, g) in vch:
+            if s in vslot:
+                n, g = vslot[s]
                 values_quant(n, g)
+                i = chunks.index((n, g))
+                if i + 1 < len(chunks):
+                    values_regroup(chunks[i + 1][0], chunks[i + 1][1])
             if 0 <= s - 3 < U:
                 readout(s - 3)

@@ -39,8 +39,8 @@ def tile_memory_pa_kernel(tc, m_in, m_out, q_in, p_m_in, p_q_in, out):
         ewp = ctx.enter_context(tc.tile_pool(name="ewp", bufs=3))
         small = ctx.enter_context(tc.tile_pool(name="small", bufs=8))
         t1p = ctx.enter_context(tc.tile_pool(name="t1p", bufs=5))
-        t2p = ctx.enter_context(tc.tile_pool(name="t2p", bufs=2))
-        osp = ctx.enter_context(tc.tile_pool(name="osp", bufs=2))
+        t2p = ctx.enter_context(tc.tile_pool(name="t2p", bufs=3))
+        osp = ctx.enter_context(tc.tile_pool(name="osp", bufs=3))
         ps_s = ctx.enter_context(tc.psum_pool(name="ps_s", bufs=3))
         ps_e = ctx.enter_context(tc.psum_pool(name="ps_e", bufs=2))
         ps_a = ctx.enter_context(tc.psum_pool(name="ps_a", bufs=1))
@@ -102,7 +102,13 @@ def tile_memory_pa_kernel(tc, m_in, m_out, q_in, p_m_in, p_q_in, out):
 
             return [one(r) for r in range(4)]
 
-        def te_steps(u):
+        def copy_on(eng, dst, src):
+            if eng == "V":
+                nc.vector.tensor_copy(out=dst, in_=src)
+            else:
+                nc.scalar.copy(out=dst, in_=src)
+
+        def te_steps(u, engines):
             def one(i):
                 def go():
                     h, k = divmod(i, 4)
@@ -116,41 +122,47 @@ def tile_memory_pa_kernel(tc, m_in, m_out, q_in, p_m_in, p_q_in, out):
                         ident_f[:],
                     )
                     if k == 3:
-                        nc.scalar.copy(
-                            out=st["eg", u][:].bitcast(F32)[:, h * 512 : (h + 1) * 512].rearrange(
+                        copy_on(
+                            engines[h],
+                            st["eg", u][:].bitcast(F32)[:, h * 512 : (h + 1) * 512].rearrange(
                                 "p (g x u) -> p g x u", g=2, u=2
                             ),
-                            in_=st["eT", u][:].rearrange("p (g u x) -> p g x u", g=2, u=2),
+                            st["eT", u][:].rearrange("p (g u x) -> p g x u", g=2, u=2),
                         )
                 return go
 
             return [one(i) for i in range(8)]
 
-        def to_steps(u):
+        def to_steps(u, engines):
             n, rest = divmod(u, 6)
             t = rest - 3
+            per = 4 // len(engines)
 
             def one(v):
                 def go():
+                    k = v % per
                     if v == 0:
+                        st["os", u] = osp.tile([P, 4, P], F32, name="os", tag="os")
+                    if k == 0:
                         st["ob", u] = ps_t.tile([P, 512], F32, name="tb", tag="tb")
-                        if t == 0:
-                            st["os", n] = osp.tile([P, 4, HW], F32, name="os", tag="os")
                     nc.tensor.transpose(
-                        st["ob", u][:, v * P : (v + 1) * P],
+                        st["ob", u][:, k * P : (k + 1) * P],
                         st["t2", u][:, v * P : (v + 1) * P],
                         ident_f[:],
                     )
-                    if v == 3:
-                        nc.scalar.copy(
-                            out=st["os", n][:, :, t * P : (t + 1) * P],
-                            in_=st["ob", u][:].rearrange("p (v x) -> p v x", v=4),
+                    if k == per - 1:
+                        copy_on(
+                            engines[v // per],
+                            st["os", u][:, v - k : v + 1, :],
+                            st["ob", u][:, : per * P].rearrange("p (v x) -> p v x", v=per),
                         )
-                        if t == XT - 1:
-                            nc.sync.dma_start(
-                                out=out[n].rearrange("(v p) h w -> p v (h w)", v=4),
-                                in_=st["os", n][:],
-                            )
+                    if v == 3:
+                        nc.sync.dma_start(
+                            out=out[n].rearrange("(v p) h w -> p v (h w)", v=4)[
+                                :, :, t * P : (t + 1) * P
+                            ],
+                            in_=st["os", u][:],
+                        )
                 return go
 
             return [one(v) for v in range(4)]
@@ -168,7 +180,7 @@ def tile_memory_pa_kernel(tc, m_in, m_out, q_in, p_m_in, p_q_in, out):
                     ib += 1
             return res
 
-        def scores(u, fill):
+        def scores(u, fill, split_exp):
             nb, t = divmod(u, XT)
             sc = scp.tile([P, CENTERS], F32, name="sc", tag="sc")
             mx4 = small.tile([P, G], F32, name="mx4", tag="mx4")
@@ -202,29 +214,48 @@ def tile_memory_pa_kernel(tc, m_in, m_out, q_in, p_m_in, p_q_in, out):
             nmx = small.tile([P, 1], F32, name="nmx", tag="nmx")
             nc.vector.tensor_reduce(out=nmx[:], in_=mx4[:], axis=AX.X, op=ALU.max, negate=True)
             e_t = ep.tile([P, CENTERS], BF16, name="e", tag="e")
-            cs = small.tile([P, 1], F32, name="cs", tag="cs")
-            nc.scalar.activation(
-                out=e_t[:], in_=sc[:], func=ACT.Exp, bias=nmx[:], scale=1.0, accum_out=cs[:]
-            )
+            parts = 2 if split_exp else 1
+            cs = small.tile([P, parts], F32, name="cs", tag="cs")
+            w = CENTERS // parts
+            for i in range(parts):
+                nc.scalar.activation(
+                    out=e_t[:, i * w : (i + 1) * w],
+                    in_=sc[:, i * w : (i + 1) * w],
+                    func=ACT.Exp,
+                    bias=nmx[:],
+                    scale=1.0,
+                    accum_out=cs[:, i : i + 1],
+                )
             st["e", u] = e_t
             st["cs", u] = cs
 
         def recip(u):
             rc = small.tile([P, 1], F32, name="rc", tag="rc")
-            nc.vector.reciprocal(out=rc[:], in_=st["cs", u][:])
+            cs = st["cs", u]
+            if cs.shape[1] > 1:
+                tot = small.tile([P, 1], F32, name="tot", tag="tot")
+                nc.vector.tensor_reduce(out=tot[:], in_=cs[:], axis=AX.X, op=ALU.add)
+                cs = tot
+            nc.vector.reciprocal(out=rc[:], in_=cs[:])
             st["rc", u] = rc
 
-        def quant_e(u):
-            ew = ewp.tile([P, 512], U32, name="ew", tag="ew", align_bytes=64)
-            es = ewp.tile([P, 512], U8, name="es", tag="es", align_bytes=64)
-            nc.vector.quantize_mx(out=ew[:].bitcast(FP8X4), scales=es[:], in_=st["eg", u][:])
-            st["ew", u] = ew
-            st["es", u] = es
+        def quant_e(u, h0, h1):
+            if h0 == 0:
+                st["ew", u] = ewp.tile([P, 512], U32, name="ew", tag="ew", align_bytes=64)
+                st["es", u] = ewp.tile([P, 512], U8, name="es", tag="es", align_bytes=64)
+            nc.vector.quantize_mx(
+                out=st["ew", u][:, h0 * 256 : h1 * 256].bitcast(FP8X4),
+                scales=st["es", u][:, h0 * 256 : h1 * 256],
+                in_=st["eg", u][:, h0 * 1024 : h1 * 1024],
+            )
 
-        def readout(u):
-            n, rest = divmod(u, 6)
-            b, t = divmod(rest, XT)
-            acc = ps_a.tile([P, VD], F32, name="acc", tag="acc")
+        def readout(u, spare_bank):
+            n = u // 6
+            if spare_bank:
+                acc = ps_s.tile([P, VD], F32, name="sb", tag="sb")
+            else:
+                acc = ps_a.tile([P, VD], F32, name="acc", tag="acc")
+            st["acc", u] = acc
             ew, es = st["ew", u], st["es", u]
             vw, vs = st["vw", n], st["vs", n]
             for g in range(G):
@@ -237,6 +268,10 @@ def tile_memory_pa_kernel(tc, m_in, m_out, q_in, p_m_in, p_q_in, out):
                     start=(g == 0),
                     stop=(g == G - 1),
                 )
+
+        def normalise(u):
+            b = (u % 6) // XT
+            acc = st["acc", u]
             if b == 0:
                 t1 = t1p.tile([P, VD], F32, name="t1", tag="t1")
                 if N1_ON_VECTOR:
@@ -316,38 +351,53 @@ def tile_memory_pa_kernel(tc, m_in, m_out, q_in, p_m_in, p_q_in, out):
         for nb in range(1, 2 * NO):
             for g in range(G):
                 tm_queue += tm_steps(nb, g, False)
-        tm_count = [8, 4, 4, 4, 6, 6]
+        tm_count = [8, 4, 4, 4, 4, 8]
         tm_pos = 0
 
-        for s in range(U + 6):
+        for s in range(U):
             if s % 3 == 0 and s // 3 + 3 < 2 * NO:
                 load_q(s // 3 + 3)
                 load_x(s // 3 + 3, 1)
             if s % 6 == 0 and s // 6 + 1 < NO:
                 alloc_r(s // 6 + 1)
                 load_r(s // 6 + 1, 0, 4)
-            fa = te_steps(s - 2) if 0 <= s - 2 < U else []
+            fa = te_steps(s - 2, ["S", "S"]) if s >= 2 else []
             fb = []
-            if 0 <= s - 4 < U and (s - 4) % 6 >= 3:
-                fb += to_steps(s - 4)
+            if s >= 5 and (s - 5) % 6 >= 3:
+                fb += to_steps(s - 5, ["S"])
             k = [0, 8, 8][s] if s < 3 else tm_count[s % 6]
             fb += tm_queue[tm_pos : tm_pos + k]
             tm_pos += k
-            fill = merge(fa, fb)
-            if s < U:
-                scores(s, fill)
-            else:
-                for f in fill:
-                    f()
-            if 0 <= s - 1 < U:
+            scores(s, merge(fa, fb), s == U - 1)
+            if s >= 1:
                 recip(s - 1)
-            if 0 <= s - 2 < U:
-                quant_e(s - 2)
+            if s >= 2:
+                quant_e(s - 2, 0, 2)
             if s in vslot:
                 n, g = vslot[s]
                 values_quant(n, g)
                 i = chunks.index((n, g))
                 if i + 1 < len(chunks):
                     values_regroup(chunks[i + 1][0], chunks[i + 1][1])
-            if 0 <= s - 3 < U:
-                readout(s - 3)
+            if s >= 3:
+                readout(s - 3, False)
+                normalise(s - 3)
+
+        for f in te_steps(U - 2, ["V", "V"]):
+            f()
+        readout(U - 3, False)
+        quant_e(U - 2, 0, 2)
+        last = te_steps(U - 1, ["V", "S"])
+        for f in last[:4]:
+            f()
+        quant_e(U - 1, 0, 1)
+        for f in last[4:]:
+            f()
+        recip(U - 1)
+        quant_e(U - 1, 1, 2)
+        readout(U - 2, True)
+        readout(U - 1, True)
+        for u in range(U - 3, U):
+            normalise(u)
+        for f in to_steps(U - 3, ["S"]) + to_steps(U - 2, ["S"]) + to_steps(U - 1, ["V", "S"]):
+            f()

@@ -45,7 +45,6 @@ def tile_memory_pa_kernel(tc, m_in, m_out, q_in, p_m_in, p_q_in, out):
         ps_e = ctx.enter_context(tc.psum_pool(name="ps_e", bufs=2))
         ps_a = ctx.enter_context(tc.psum_pool(name="ps_a", bufs=1))
         ps_t = ctx.enter_context(tc.psum_pool(name="ps_t", bufs=2))
-        ctx.enter_context(tc.manual_schedule())
 
         st = {}
 

from contextlib import ExitStack

import concourse.mybir as mybir
from concourse.masks import make_identity

F32 = mybir.dt.float32
BF16 = mybir.dt.bfloat16
U32 = mybir.dt.uint32
U8 = mybir.dt.uint8
FP8X4 = mybir.dt.float8_e4m3fn_x4
ALU = mybir.AluOpType
ACT = mybir.ActivationFunctionType
AX = mybir.AxisListType

P = 128
NO, CENTERS, C, VD, HW = 4, 2048, 256, 512, 384
G = CENTERS // 512
XT = HW // P
U = NO * 2 * XT
FLOPS = 2 * NO * 2 * CENTERS * C * HW + 2 * NO * 2 * VD * CENTERS * HW
VALUES_ON_GPSIMD = True
N1_ON_VECTOR = True


def tile_memory_pa_kernel(tc, m_in, m_out, q_in, p_m_in, p_q_in, out):
    nc = tc.nc
    keys = [m_in, p_m_in]
    queries = [q_in, p_q_in]
    with ExitStack() as ctx:
        const = ctx.enter_context(tc.tile_pool(name="const", bufs=1))
        xin = ctx.enter_context(tc.tile_pool(name="xin", bufs=3))
        tpool = ctx.enter_context(tc.tile_pool(name="tpool", bufs=2))
        rpool = ctx.enter_context(tc.tile_pool(name="rpool", bufs=2))
        vgp = ctx.enter_context(tc.tile_pool(name="vgp", bufs=1))
        vwp = ctx.enter_context(tc.tile_pool(name="vwp", bufs=2))
        scp = ctx.enter_context(tc.tile_pool(name="scp", bufs=3))
        ep = ctx.enter_context(tc.tile_pool(name="ep", bufs=3))
        egp = ctx.enter_context(tc.tile_pool(name="egp", bufs=2))
        ewp = ctx.enter_context(tc.tile_pool(name="ewp", bufs=3))
        small = ctx.enter_context(tc.tile_pool(name="small", bufs=8))
        t1p = ctx.enter_context(tc.tile_pool(name="t1p", bufs=5))
        t2p = ctx.enter_context(tc.tile_pool(name="t2p", bufs=3))
        osp = ctx.enter_context(tc.tile_pool(name="osp", bufs=3))
        ps_s = ctx.enter_context(tc.psum_pool(name="ps_s", bufs=3))
        ps_e = ctx.enter_context(tc.psum_pool(name="ps_e", bufs=2))
        ps_a = ctx.enter_context(tc.psum_pool(name="ps_a", bufs=1))
        ps_t = ctx.enter_context(tc.psum_pool(name="ps_t", bufs=2))

        st = {}

        def load_q(nb):
            n, b = divmod(nb, 2)
            q = const.tile([P, 2, HW], BF16, name="q%d" % nb)
            nc.sync.dma_start(out=q[:], in_=queries[b][n].rearrange("(w e) h v -> w e (h v)", e=2))
            st["q", nb] = q

        def load_x(nb, pieces):
            n, b = divmod(nb, 2)
            x = xin.tile([P, G * 1024], BF16, name="x", tag="x")
            src = keys[b][n].rearrange("(g j r) c -> j g (r c)", g=G, r=4)
            dst = x[:].rearrange("j (g k) -> j g k", g=G)
            step = G // pieces
            for i in range(pieces):
                nc.sync.dma_start(
                    out=dst[:, i * step : (i + 1) * step, :], in_=src[:, i * step : (i + 1) * step, :]
                )
            st["x", nb] = x

        def alloc_r(n):
            st["r", n] = rpool.tile([P, G * 2048], BF16, name="r", tag="r")

        def load_r(n, g0, g1):
            nc.sync.dma_start(
                out=st["r", n][:].rearrange("p (g k) -> p g k", g=G)[:, g0:g1, :],
                in_=m_out[n].rearrange("(g p t) w -> p g (t w)", g=G, t=4)[:, g0:g1, :],
            )

        def tm_steps(nb, g, on_vector):
            def one(r):
                def go():
                    if r == 0:
                        if g == 0:
                            st["T", nb] = tpool.tile([P, CENTERS], F32, name="T", tag="T")
                        st["tmb", nb] = ps_t.tile([P, 512], F32, name="tb", tag="tb")
                    xw = st["x", nb][:].bitcast(F32)
                    nc.tensor.transpose(
                        st["tmb", nb][:, r * P : (r + 1) * P],
                        xw[:, (g * 4 + r) * P : (g * 4 + r + 1) * P],
                        ident_f[:],
                    )
                    if r == 3:
                        dst = st["T", nb][:, g * 512 : (g + 1) * 512].rearrange(
                            "w (u j e) -> w u j e", u=2, e=2
                        )
                        src = st["tmb", nb][:].rearrange("w (u e j) -> w u j e", u=2, e=2)
                        if on_vector:
                            nc.vector.tensor_copy(out=dst, in_=src)
                        else:
                            nc.scalar.copy(out=dst, in_=src)
                return go

            return [one(r) for r in range(4)]

        def copy_on(eng, dst, src):
            if eng == "V":
                nc.vector.tensor_copy(out=dst, in_=src)
            else:
                nc.scalar.copy(out=dst, in_=src)

        def te_steps(u, engines):
            def one(i):
                def go():
                    h, k = divmod(i, 4)
                    if i == 0:
                        st["eg", u] = egp.tile([P, 2048], BF16, name="eg", tag="eg", align_bytes=64)
                    if k == 0:
                        st["eT", u] = ps_e.tile([P, 512], F32, name="eT", tag="eT")
                    nc.tensor.transpose(
                        st["eT", u][:, k * P : (k + 1) * P],
                        st["e", u][:].bitcast(F32)[:, i * P : (i + 1) * P],
                        ident_f[:],
                    )
                    if k == 3:
                        copy_on(
                            engines[h],
                            st["eg", u][:].bitcast(F32)[:, h * 512 : (h + 1) * 512].rearrange(
                                "p (g x u) -> p g x u", g=2, u=2
                            ),
                            st["eT", u][:].rearrange("p (g u x) -> p g x u", g=2, u=2),
                        )
                return go

            return [one(i) for i in range(8)]

        def to_steps(u, engines):
            n, rest = divmod(u, 6)
            t = rest - 3
            per = 4 // len(engines)

            def one(v):
                def go():
                    k = v % per
                    if v == 0:
                        st["os", u] = osp.tile([P, 4, P], F32, name="os", tag="os")
                    if k == 0:
                        st["ob", u] = ps_t.tile([P, 512], F32, name="tb", tag="tb")
                    nc.tensor.transpose(
                        st["ob", u][:, k * P : (k + 1) * P],
                        st["t2", u][:, v * P : (v + 1) * P],
                        ident_f[:],
                    )
                    if k == per - 1:
                        copy_on(
                            engines[v // per],
                            st["os", u][:, v - k : v + 1, :],
                            st["ob", u][:, : per * P].rearrange("p (v x) -> p v x", v=per),
                        )
                    if v == 3:
                        nc.sync.dma_start(
                            out=out[n].rearrange("(v p) h w -> p v (h w)", v=4)[
                                :, :, t * P : (t + 1) * P
                            ],
                            in_=st["os", u][:],
                        )
                return go

            return [one(v) for v in range(4)]

        def merge(a, b):
            res = []
            na, nb_ = len(a), len(b)
            ia = ib = 0
            while ia < na or ib < nb_:
                if ib >= nb_ or (ia < na and ia * nb_ <= ib * na):
                    res.append(a[ia])
                    ia += 1
                else:
                    res.append(b[ib])
                    ib += 1
            return res

        def scores(u, fill, split_exp):
            nb, t = divmod(u, XT)
            sc = scp.tile([P, CENTERS], F32, name="sc", tag="sc")
            mx4 = small.tile([P, G], F32, name="mx4", tag="mx4")
            t2v = st["T", nb][:].bitcast(BF16).rearrange("w (k e) -> w k e", e=2)
            q = st["q", nb]
            gaps = 2 * G - 1
            for g in range(G):
                bank = ps_s.tile([P, 512], F32, name="sb", tag="sb")
                for e in range(2):
                    nc.tensor.matmul(
                        out=bank[:],
                        lhsT=q[:, e, t * P : (t + 1) * P],
                        rhs=t2v[:, g * 512 : (g + 1) * 512, e],
                        start=(e == 0),
                        stop=(e == 1),
                    )
                    if e == 1:
                        nc.vector.tensor_scalar(
                            out=sc[:, g * 512 : (g + 1) * 512],
                            in0=bank[:],
                            scalar1=1.0 / 16.0,
                            scalar2=None,
                            op0=ALU.mult,
                            op1=ALU.max,
                            accum_out=mx4[:, g : g + 1],
                        )
                    i = 2 * g + e
                    if i < gaps:
                        for f in fill[i * len(fill) // gaps : (i + 1) * len(fill) // gaps]:
                            f()
            nmx = small.tile([P, 1], F32, name="nmx", tag="nmx")
            nc.vector.tensor_reduce(out=nmx[:], in_=mx4[:], axis=AX.X, op=ALU.max, negate=True)
            e_t = ep.tile([P, CENTERS], BF16, name="e", tag="e")
            parts = 2 if split_exp else 1
            cs = small.tile([P, parts], F32, name="cs", tag="cs")
            w = CENTERS // parts
            for i in range(parts):
                nc.scalar.activation(
                    out=e_t[:, i * w : (i + 1) * w],
                    in_=sc[:, i * w : (i + 1) * w],
                    func=ACT.Exp,
                    bias=nmx[:],
                    scale=1.0,
                    accum_out=cs[:, i : i + 1],
                )
            st["e", u] = e_t
            st["cs", u] = cs

        def recip(u):
            rc = small.tile([P, 1], F32, name="rc", tag="rc")
            cs = st["cs", u]
            if cs.shape[1] > 1:
                tot = small.tile([P, 1], F32, name="tot", tag="tot")
                nc.vector.tensor_reduce(out=tot[:], in_=cs[:], axis=AX.X, op=ALU.add)
                cs = tot
            nc.vector.reciprocal(out=rc[:], in_=cs[:])
            st["rc", u] = rc

        def quant_e(u, h0, h1):
            if h0 == 0:
                st["ew", u] = ewp.tile([P, 512], U32, name="ew", tag="ew", align_bytes=64)
                st["es", u] = ewp.tile([P, 512], U8, name="es", tag="es", align_bytes=64)
            nc.vector.quantize_mx(
                out=st["ew", u][:, h0 * 256 : h1 * 256].bitcast(FP8X4),
                scales=st["es", u][:, h0 * 256 : h1 * 256],
                in_=st["eg", u][:, h0 * 1024 : h1 * 1024],
            )

        def readout(u, spare_bank):
            n = u // 6
            if spare_bank:
                acc = ps_s.tile([P, VD], F32, name="sb", tag="sb")
            else:
                acc = ps_a.tile([P, VD], F32, name="acc", tag="acc")
            st["acc", u] = acc
            ew, es = st["ew", u], st["es", u]
            vw, vs = st["vw", n], st["vs", n]
            for g in range(G):
                nc.tensor.matmul_mx(
                    out=acc[:],
                    lhsT=ew[:, g * P : (g + 1) * P].bitcast(FP8X4),
                    lhsT_scale=es[:, g * P : (g + 1) * P],
                    rhs=vw[:, g * 512 : (g + 1) * 512].bitcast(FP8X4),
                    rhs_scale=vs[:, g * 512 : (g + 1) * 512],
                    start=(g == 0),
                    stop=(g == G - 1),
                )

        def normalise(u):
            b = (u % 6) // XT
            acc = st["acc", u]
            if b == 0:
                t1 = t1p.tile([P, VD], F32, name="t1", tag="t1")
                if N1_ON_VECTOR:
                    nc.vector.tensor_scalar(
                        out=t1[:], in0=acc[:], scalar1=st["rc", u][:], scalar2=None, op0=ALU.mult
                    )
                else:
                    nc.scalar.activation(out=t1[:], in_=acc[:], func=ACT.Copy, scale=st["rc", u][:])
                st["t1", u] = t1
            else:
                t2 = t2p.tile([P, VD], F32, name="t2", tag="t2")
                nc.vector.scalar_tensor_tensor(
                    out=t2[:],
                    in0=acc[:],
                    scalar=st["rc", u][:],
                    in1=st["t1", u - XT][:],
                    op0=ALU.mult,
                    op1=ALU.add,
                )
                st["t2", u] = t2

        def values_regroup(n, g):
            vg = vgp.tile([P, 2048], BF16, name="vg", tag="vg", align_bytes=64)
            if VALUES_ON_GPSIMD:
                nc.gpsimd.tensor_scalar(
                    out=vg[:].rearrange("p (w t) -> p w t", t=4),
                    in0=st["r", n][:, g * 2048 : (g + 1) * 2048].rearrange("p (t w) -> p w t", t=4),
                    scalar1=1.0,
                    scalar2=0.0,
                    op0=ALU.mult,
                    op1=ALU.add,
                )
            else:
                nc.vector.tensor_copy(
                    out=vg[:].rearrange("p (c i t) -> p c t i", i=4, t=4),
                    in_=st["r", n][:, g * 2048 : (g + 1) * 2048].rearrange(
                        "p (t c i) -> p c t i", t=4, i=4
                    ),
                )
            st["vg", n, g] = vg

        def values_quant(n, g):
            if g == 0:
                st["vw", n] = vwp.tile([P, G * 512], U32, name="vw", tag="vw", align_bytes=64)
                st["vs", n] = vwp.tile([P, G * 512], U8, name="vs", tag="vs", align_bytes=64)
            nc.vector.quantize_mx(
                out=st["vw", n][:, g * 512 : (g + 1) * 512].bitcast(FP8X4),
                scales=st["vs", n][:, g * 512 : (g + 1) * 512],
                in_=st["vg", n, g][:],
            )

        vslot = {}
        chunks = [(n, g) for n in range(NO) for g in range(G)]
        for (n, g) in chunks:
            vslot[6 * n - 2 + g if n > 0 else g] = (n, g)

        load_q(0)
        load_x(0, 4)
        alloc_r(0)
        load_r(0, 0, 1)
        load_q(1)
        load_x(1, 2)
        load_r(0, 1, 4)
        load_q(2)
        load_x(2, 1)
        ident_f = const.tile([P, P], F32, name="ident_f")
        make_identity(nc, ident_f[:])
        warm = const.tile([P, 8], F32, name="warm")
        nc.vector.memset(warm[:], 0.0)
        nc.scalar.activation(out=warm[:], in_=warm[:], func=ACT.Exp)
        for g in range(G):
            for f in tm_steps(0, g, g % 2 == 0):
                f()
        values_regroup(0, 0)

        tm_queue = []
        for nb in range(1, 2 * NO):
            for g in range(G):
                tm_queue += tm_steps(nb, g, False)
        tm_count = [8, 4, 4, 4, 4, 8]
        tm_pos = 0

        for s in range(U):
            if s % 3 == 0 and s // 3 + 3 < 2 * NO:
                load_q(s // 3 + 3)
                load_x(s // 3 + 3, 1)
            if s % 6 == 0 and s // 6 + 1 < NO:
                alloc_r(s // 6 + 1)
                load_r(s // 6 + 1, 0, 4)
            fa = te_steps(s - 2, ["S", "S"]) if s >= 2 else []
            fb = []
            if s >= 5 and (s - 5) % 6 >= 3:
                fb += to_steps(s - 5, ["S"])
            k = [0, 8, 8][s] if s < 3 else tm_count[s % 6]
            fb += tm_queue[tm_pos : tm_pos + k]
            tm_pos += k
            scores(s, merge(fa, fb), s == U - 1)
            if s >= 1:
                recip(s - 1)
            if s >= 2:
                quant_e(s - 2, 0, 2)
            if s in vslot:
                n, g = vslot[s]
                values_quant(n, g)
                i = chunks.index((n, g))
                if i + 1 < len(chunks):
                    values_regroup(chunks[i + 1][0], chunks[i + 1][1])
            if s >= 3:
                readout(s - 3, False)
                normalise(s - 3)

        for f in te_steps(U - 2, ["V", "V"]):
            f()
        readout(U - 3, False)
        quant_e(U - 2, 0, 2)
        last = te_steps(U - 1, ["V", "S"])
        for f in last[:4]:
            f()
        quant_e(U - 1, 0, 1)
        for f in last[4:]:
            f()
        recip(U - 1)
        quant_e(U - 1, 1, 2)
        readout(U - 2, True)
        readout(U - 1, True)
        for u in range(U - 3, U):
            normalise(u)
        for f in to_steps(U - 3, ["S"]) + to_steps(U - 2, ["S"]) + to_steps(U - 1, ["V", "S"]):
            f()
